import numpy as np
import ml_dtypes


def mxq(x, axis, fmt="e4m3"):
    dtype, down = {"e4m3": (ml_dtypes.float8_e4m3fn, 7), "e5m2": (ml_dtypes.float8_e5m2, 14)}[fmt]
    v = np.moveaxis(np.asarray(x, np.float32).astype(ml_dtypes.bfloat16).astype(np.float64), axis, -1)
    blocks = v.reshape(v.shape[:-1] + (-1, 32))
    amax = np.abs(blocks).max(-1, keepdims=True)
    byte = np.maximum(np.where(amax > 0, np.frexp(amax)[1] - 1 + 127, 0) - down, 1)
    scale = np.exp2(byte - 127.0)
    codes = (blocks / scale).astype(np.float32).astype(dtype).astype(np.float64)
    return np.moveaxis((codes * scale).reshape(v.shape), -1, axis)


WIDE = False


def mx_kscale(k):
    if not WIDE:
        return np.ones(k)
    levels = np.array([10, -10, 5, -5, 0])
    a = np.random.permutation(np.resize(levels, k // 512 * 4)).reshape(k // 512, 4)
    idx = np.arange(k)
    return np.exp2(a[idx // 512, idx % 128 // 32])


BF16 = ml_dtypes.bfloat16


def bf(x):
    return np.asarray(x, np.float32).astype(BF16)


def f64(x):
    return np.asarray(x).astype(np.float64)


B, C, O, H, W, P, Q = 2, 4096, 256, 16, 16, 4, 4
PMAX = max(P, Q)
HW = H * W


def order_rms(n):
    return np.sqrt(np.array([np.prod(np.arange(1.0, 2.0 * i, 2.0)) for i in range(1, n + 1)]))[:, None, None]


def kpow(s, n):
    return np.exp2(np.log2(s)[None, None, :] * np.arange(1, n + 1)[:, None, None])


def setup_inputs():
    s = mx_kscale(C)
    return {"x": bf(np.random.standard_normal((B, C, H, W)) * s[None, :, None, None]),
            "Wp": bf(np.random.standard_normal((P, O, C)) / (np.sqrt(C) * order_rms(P)) / kpow(s, P)),
            "bp": bf(np.random.standard_normal(O) * 0.5),
            "Wq": bf(np.random.standard_normal((Q, O, C)) / (np.sqrt(C) * order_rms(Q)) / kpow(s, Q))}


def reference(x, Wp, bp, Wq):
    x = f64(x)
    pows = [x]
    for _ in range(PMAX - 1):
        pows.append(pows[-1] * x)
    Xs = np.stack(pows, axis=0)
    Xr = Xs.reshape(PMAX, B, C, HW).transpose(1, 3, 0, 2).reshape(B * HW, PMAX * C)
    Xq = mxq(Xr, 1, "e4m3")
    Wpq = mxq(f64(Wp).transpose(0, 2, 1).reshape(P * C, O), 0, "e4m3")
    Wqq = mxq(f64(Wq).transpose(0, 2, 1).reshape(Q * C, O), 0, "e4m3")
    sum_p = (Xq[:, :P * C] @ Wpq) + f64(bp)[None, :]
    sum_q = Xq[:, :Q * C] @ Wqq
    out = sum_p / (1.0 + np.abs(sum_q))
    return np.ascontiguousarray(out.reshape(B, H, W, O).transpose(0, 3, 1, 2))

@@ -1,0 +1,190 @@
+from contextlib import ExitStack
+
+import concourse.mybir as mybir
+from concourse.masks import make_identity
+
+F32 = mybir.dt.float32
+BF16 = mybir.dt.bfloat16
+U32 = mybir.dt.uint32
+U8 = mybir.dt.uint8
+FP8X4 = mybir.dt.float8_e4m3fn_x4
+ACT = mybir.ActivationFunctionType
+ALU = mybir.AluOpType
+
+BATCH, CHANNELS, OUT_CH, PIXELS, ORDERS = 2, 4096, 256, 256, 4
+P = 128
+PACK = 4
+K_PASS = P * PACK
+GROUPS = CHANNELS // K_PASS
+N = BATCH * PIXELS
+O_TILES = OUT_CH // P
+GROUPED = N * PACK
+W_ROWS = ORDERS * O_TILES
+HALF_STEPS = 2 * GROUPS
+
+FLOPS = 2 * 2 * N * OUT_CH * ORDERS * CHANNELS
+
+
+def tile_kanvolutionlayer_k_kernel(tc, x, Wp, bp, Wq, out):
+    nc = tc.nc
+    x_view = x.rearrange("b (g u p e) h w -> b g p u (e h w)", g=GROUPS, u=2, p=P, e=2)
+    w_views = [
+        Wq.rearrange("i (t o) c -> o (i t) c", o=P),
+        Wp.rearrange("i (t o) c -> o (i t) c", o=P),
+    ]
+    out_view = out.rearrange("b (t o) h w -> t o b (h w)", o=P)
+
+    with ExitStack() as ctx:
+        const = ctx.enter_context(tc.tile_pool(name="const", bufs=1))
+        x_in = ctx.enter_context(tc.tile_pool(name="x_in", bufs=3))
+        w_in = ctx.enter_context(tc.tile_pool(name="w_in", bufs=6))
+        powers = ctx.enter_context(tc.tile_pool(name="powers", bufs=2))
+        x_mx = ctx.enter_context(tc.tile_pool(name="x_mx", bufs=3))
+        w_mx = ctx.enter_context(tc.tile_pool(name="w_mx", bufs=3))
+        tail = ctx.enter_context(tc.tile_pool(name="tail", bufs=2))
+        sums = ctx.enter_context(tc.psum_pool(name="sums", bufs=1))
+        turned = ctx.enter_context(tc.psum_pool(name="turned", bufs=4))
+
+        ident = const.tile([P, P], F32)
+        make_identity(nc, ident[:])
+        bias_bf = const.tile([P, O_TILES], BF16)
+        with nc.allow_non_contiguous_dma(reason="256 bias values, one to a partition"):
+            nc.scalar.dma_start(out=bias_bf[:], in_=bp.rearrange("(t o) -> o t", o=P))
+        bias = const.tile([P, O_TILES], F32)
+        nc.vector.tensor_copy(out=bias[:], in_=bias_bf[:])
+
+        acc = [
+            [sums.tile([P, N], F32, name="acc_%d_%d" % (s, t)) for t in range(O_TILES)]
+            for s in range(2)
+        ]
+
+        x_raw, w_raw = {}, {}
+        x_low, x_high, x_sq = {}, {}, {}
+        x_codes, x_scales = {}, {}
+        w_codes, w_scales, w_grouped = {}, {}, {}
+
+        def load_x(g):
+            x_raw[g] = x_in.tile([P, BATCH, PACK, PIXELS], BF16, name="x_raw")
+            for b in range(BATCH):
+                nc.sync.dma_start(
+                    out=x_raw[g][:, b].rearrange("p (u e) w -> p u (e w)", u=2),
+                    in_=x_view[b, g],
+                )
+
+        def load_w(h):
+            g, s = h // 2, h % 2
+            w_raw[h] = w_in.tile([P, W_ROWS, K_PASS], BF16, name="w_raw")
+            nc.sync.dma_start(out=w_raw[h][:], in_=w_views[s][:, :, g * K_PASS : (g + 1) * K_PASS])
+
+        def powers_low(g):
+            x_low[g] = powers.tile([P, 2 * GROUPED], BF16, name="x_low", align_bytes=64)
+            x_sq[g] = powers.tile([P, GROUPED], F32, name="x_sq")
+            x1 = x_low[g][:, 0:GROUPED]
+            nc.vector.tensor_copy(
+                out=x1.rearrange("p (b w t) -> p b w t", b=BATCH, t=PACK),
+                in_=x_raw[g][:].rearrange("p b t w -> p b w t"),
+            )
+            nc.scalar.activation(out=x_sq[g][:], in_=x1, func=ACT.Square)
+            nc.vector.tensor_tensor(out=x_low[g][:, GROUPED:], in0=x1, in1=x1, op=ALU.mult)
+
+        def powers_high(g):
+            x_high[g] = powers.tile([P, 2 * GROUPED], BF16, name="x_high", align_bytes=64)
+            nc.scalar.activation(out=x_high[g][:, GROUPED:], in_=x_sq[g][:], func=ACT.Square)
+            nc.vector.tensor_tensor(
+                out=x_high[g][:, 0:GROUPED], in0=x_sq[g][:], in1=x_low[g][:, 0:GROUPED], op=ALU.mult
+            )
+
+        def quantise_x(g, half, src):
+            if half == 0:
+                x_codes[g] = x_mx.tile([P, ORDERS * N], U32, name="x_codes", align_bytes=64)
+                x_scales[g] = x_mx.tile([P, ORDERS * N], U8, name="x_scales", align_bytes=64)
+            cols = slice(half * 2 * N, (half + 1) * 2 * N)
+            nc.vector.quantize_mx(
+                out=x_codes[g][:, cols].bitcast(FP8X4), scales=x_scales[g][:, cols], in_=src[:]
+            )
+
+        def turn_w(h):
+            words = w_raw[h][:].bitcast(F32)
+            w_grouped[h] = w_mx.tile([P, W_ROWS * P * PACK], BF16, name="w_grouped", align_bytes=64)
+            grouped_words = w_grouped[h][:].bitcast(F32)
+            for i in range(ORDERS):
+                bank = turned.tile([P, O_TILES, 2, P], F32, name="bank")
+                for t in range(O_TILES):
+                    for u in range(2):
+                        nc.tensor.transpose(
+                            bank[:, t, u, :], words[:, i * O_TILES + t, u * P : (u + 1) * P], ident[:]
+                        )
+                nc.scalar.copy(
+                    out=grouped_words[:, i * N : (i + 1) * N].rearrange(
+                        "p (t o u) -> p t o u", t=O_TILES, u=2
+                    ),
+                    in_=bank[:].rearrange("p t u o -> p t o u"),
+                )
+
+        def quantise_w(h):
+            w_codes[h] = w_mx.tile([P, W_ROWS * P], U32, name="w_codes", align_bytes=64)
+            w_scales[h] = w_mx.tile([P, W_ROWS * P], U8, name="w_scales", align_bytes=64)
+            nc.vector.quantize_mx(
+                out=w_codes[h][:].bitcast(FP8X4), scales=w_scales[h][:], in_=w_grouped[h][:]
+            )
+
+        def multiply(h):
+            g, s = h // 2, h % 2
+            for t in range(O_TILES):
+                for i in range(ORDERS):
+                    o_cols = slice((i * O_TILES + t) * P, (i * O_TILES + t + 1) * P)
+                    n_cols = slice(i * N, (i + 1) * N)
+                    nc.tensor.matmul_mx(
+                        out=acc[s][t][:],
+                        lhsT=w_codes[h][:, o_cols].bitcast(FP8X4),
+                        lhsT_scale=w_scales[h][:, o_cols],
+                        rhs=x_codes[g][:, n_cols].bitcast(FP8X4),
+                        rhs_scale=x_scales[g][:, n_cols],
+                        start=(g == 0 and i == 0),
+                        stop=(g == GROUPS - 1 and i == ORDERS - 1),
+                    )
+
+        load_x(0)
+        load_w(0)
+        load_w(1)
+        load_x(1)
+        load_w(2)
+        load_w(3)
+        powers_low(0)
+        for h in range(HALF_STEPS + 1):
+            g = h // 2
+            if h % 2 == 0 and g + 2 < GROUPS:
+                load_x(g + 2)
+            if h + 4 < HALF_STEPS:
+                load_w(h + 4)
+            if h < HALF_STEPS:
+                turn_w(h)
+            if h >= 1:
+                quantise_w(h - 1)
+            if h % 2 == 0 and g < GROUPS:
+                quantise_x(g, 0, x_low[g])
+                powers_high(g)
+            if h % 2 == 1:
+                quantise_x(g, 1, x_high[g])
+                if g + 1 < GROUPS:
+                    powers_low(g + 1)
+            if h >= 1:
+                multiply(h - 1)
+
+        for t in range(O_TILES):
+            size = tail.tile([P, N], F32, name="size")
+            nc.scalar.activation(out=size[:], in_=acc[0][t][:], func=ACT.Abs)
+            root = tail.tile([P, N], F32, name="root")
+            nc.scalar.activation(out=root[:], in_=size[:], func=ACT.Abs_reciprocal_sqrt, bias=1.0)
+            inverse = tail.tile([P, N], F32, name="inverse")
+            nc.scalar.activation(out=inverse[:], in_=root[:], func=ACT.Square)
+            result = tail.tile([P, N], F32, name="result")
+            nc.vector.scalar_tensor_tensor(
+                out=result[:],
+                in0=acc[1][t][:],
+                scalar=bias[:, t : t + 1],
+                in1=inverse[:],
+                op0=ALU.add,
+                op1=ALU.mult,
+            )
+            nc.sync.dma_start(out=out_view[t], in_=result[:].rearrange("p (b w) -> p b w", b=BATCH))

@@ -20,7 +20,7 @@ N = BATCH * PIXELS
 O_TILES = OUT_CH // P
 GROUPED = N * PACK
 W_ROWS = ORDERS * O_TILES
-HALF_STEPS = 2 * GROUPS
+CHUNKS = 2 * GROUPS
 
 FLOPS = 2 * 2 * N * OUT_CH * ORDERS * CHANNELS
 
@@ -44,14 +44,7 @@ def tile_kanvolutionlayer_k_kernel(tc, x, Wp, bp, Wq, out):
         tail = ctx.enter_context(tc.tile_pool(name="tail", bufs=2))
         sums = ctx.enter_context(tc.psum_pool(name="sums", bufs=1))
         turned = ctx.enter_context(tc.psum_pool(name="turned", bufs=4))
-
-        ident = const.tile([P, P], F32)
-        make_identity(nc, ident[:])
-        bias_bf = const.tile([P, O_TILES], BF16)
-        with nc.allow_non_contiguous_dma(reason="256 bias values, one to a partition"):
-            nc.scalar.dma_start(out=bias_bf[:], in_=bp.rearrange("(t o) -> o t", o=P))
-        bias = const.tile([P, O_TILES], F32)
-        nc.vector.tensor_copy(out=bias[:], in_=bias_bf[:])
+        ctx.enter_context(tc.manual_schedule())
 
         acc = [
             [sums.tile([P, N], F32, name="acc_%d_%d" % (s, t)) for t in range(O_TILES)]
@@ -62,6 +55,7 @@ def tile_kanvolutionlayer_k_kernel(tc, x, Wp, bp, Wq, out):
         x_low, x_high, x_sq = {}, {}, {}
         x_codes, x_scales = {}, {}
         w_codes, w_scales, w_grouped = {}, {}, {}
+        inverse = {}
 
         def load_x(g):
             x_raw[g] = x_in.tile([P, BATCH, PACK, PIXELS], BF16, name="x_raw")
@@ -76,31 +70,50 @@ def tile_kanvolutionlayer_k_kernel(tc, x, Wp, bp, Wq, out):
             w_raw[h] = w_in.tile([P, W_ROWS, K_PASS], BF16, name="w_raw")
             nc.sync.dma_start(out=w_raw[h][:], in_=w_views[s][:, :, g * K_PASS : (g + 1) * K_PASS])
 
-        def powers_low(g):
+        def load_group(g):
+            if g + 1 < GROUPS:
+                load_x(g + 1)
+            load_w(2 * g)
+            load_w(2 * g + 1)
+
+        def regroup_x(g):
             x_low[g] = powers.tile([P, 2 * GROUPED], BF16, name="x_low", align_bytes=64)
-            x_sq[g] = powers.tile([P, GROUPED], F32, name="x_sq")
-            x1 = x_low[g][:, 0:GROUPED]
             nc.vector.tensor_copy(
-                out=x1.rearrange("p (b w t) -> p b w t", b=BATCH, t=PACK),
+                out=x_low[g][:, 0:GROUPED].rearrange("p (b w t) -> p b w t", b=BATCH, t=PACK),
                 in_=x_raw[g][:].rearrange("p b t w -> p b w t"),
             )
-            nc.scalar.activation(out=x_sq[g][:], in_=x1, func=ACT.Square)
+
+        def square_f32(g):
+            x_sq[g] = powers.tile([P, GROUPED], F32, name="x_sq")
+            nc.scalar.activation(out=x_sq[g][:], in_=x_low[g][:, 0:GROUPED], func=ACT.Square)
+
+        def square_bf16(g):
+            x1 = x_low[g][:, 0:GROUPED]
             nc.vector.tensor_tensor(out=x_low[g][:, GROUPED:], in0=x1, in1=x1, op=ALU.mult)
 
-        def powers_high(g):
+        def fourth(g):
             x_high[g] = powers.tile([P, 2 * GROUPED], BF16, name="x_high", align_bytes=64)
             nc.scalar.activation(out=x_high[g][:, GROUPED:], in_=x_sq[g][:], func=ACT.Square)
+
+        def cube(g):
             nc.vector.tensor_tensor(
                 out=x_high[g][:, 0:GROUPED], in0=x_sq[g][:], in1=x_low[g][:, 0:GROUPED], op=ALU.mult
             )
 
-        def quantise_x(g, half, src):
-            if half == 0:
-                x_codes[g] = x_mx.tile([P, ORDERS * N], U32, name="x_codes", align_bytes=64)
-                x_scales[g] = x_mx.tile([P, ORDERS * N], U8, name="x_scales", align_bytes=64)
-            cols = slice(half * 2 * N, (half + 1) * 2 * N)
+        def quantise_x_low(g):
+            x_codes[g] = x_mx.tile([P, ORDERS * N], U32, name="x_codes", align_bytes=64)
+            x_scales[g] = x_mx.tile([P, ORDERS * N], U8, name="x_scales", align_bytes=64)
             nc.vector.quantize_mx(
-                out=x_codes[g][:, cols].bitcast(FP8X4), scales=x_scales[g][:, cols], in_=src[:]
+                out=x_codes[g][:, 0 : 2 * N].bitcast(FP8X4),
+                scales=x_scales[g][:, 0 : 2 * N],
+                in_=x_low[g][:],
+            )
+
+        def quantise_x_high(g):
+            nc.vector.quantize_mx(
+                out=x_codes[g][:, 2 * N :].bitcast(FP8X4),
+                scales=x_scales[g][:, 2 * N :],
+                in_=x_high[g][:],
             )
 
         def turn_w(h):
@@ -144,47 +157,76 @@ def tile_kanvolutionlayer_k_kernel(tc, x, Wp, bp, Wq, out):
                         stop=(g == GROUPS - 1 and i == ORDERS - 1),
                     )
 
-        load_x(0)
-        load_w(0)
-        load_w(1)
-        load_x(1)
-        load_w(2)
-        load_w(3)
-        powers_low(0)
-        for h in range(HALF_STEPS + 1):
-            g = h // 2
-            if h % 2 == 0 and g + 2 < GROUPS:
-                load_x(g + 2)
-            if h + 4 < HALF_STEPS:
-                load_w(h + 4)
-            if h < HALF_STEPS:
-                turn_w(h)
-            if h >= 1:
-                quantise_w(h - 1)
-            if h % 2 == 0 and g < GROUPS:
-                quantise_x(g, 0, x_low[g])
-                powers_high(g)
-            if h % 2 == 1:
-                quantise_x(g, 1, x_high[g])
-                if g + 1 < GROUPS:
-                    powers_low(g + 1)
-            if h >= 1:
-                multiply(h - 1)
-
-        for t in range(O_TILES):
+        def invert_denominator(t):
             size = tail.tile([P, N], F32, name="size")
             nc.scalar.activation(out=size[:], in_=acc[0][t][:], func=ACT.Abs)
             root = tail.tile([P, N], F32, name="root")
             nc.scalar.activation(out=root[:], in_=size[:], func=ACT.Abs_reciprocal_sqrt, bias=1.0)
-            inverse = tail.tile([P, N], F32, name="inverse")
-            nc.scalar.activation(out=inverse[:], in_=root[:], func=ACT.Square)
+            inverse[t] = tail.tile([P, N], F32, name="inverse")
+            nc.vector.tensor_tensor(out=inverse[t][:], in0=root[:], in1=root[:], op=ALU.mult)
+
+        def finish(t):
             result = tail.tile([P, N], F32, name="result")
             nc.vector.scalar_tensor_tensor(
                 out=result[:],
                 in0=acc[1][t][:],
                 scalar=bias[:, t : t + 1],
-                in1=inverse[:],
+                in1=inverse[t][:],
                 op0=ALU.add,
                 op1=ALU.mult,
             )
             nc.sync.dma_start(out=out_view[t], in_=result[:].rearrange("p (b w) -> p b w", b=BATCH))
+
+        load_x(0)
+        load_group(0)
+        load_group(1)
+
+        ident = const.tile([P, P], F32)
+        make_identity(nc, ident[:])
+        bias_bf = const.tile([P, O_TILES], BF16)
+        with nc.allow_non_contiguous_dma(reason="256 bias values, one to a partition"):
+            nc.scalar.dma_start(out=bias_bf[:], in_=bp.rearrange("(t o) -> o t", o=P))
+        ones = const.tile([P, 1], F32)
+        nc.vector.memset(ones[:], 1.0)
+        warm = const.tile([P, 1], F32)
+        nc.scalar.activation(out=warm[:], in_=ones[:], func=ACT.Abs_reciprocal_sqrt)
+
+        regroup_x(0)
+        for step in range(-1, CHUNKS + 2):
+            g = (step + 1) // 2
+            odd = step % 2 == 1
+            if not odd and g + 2 < GROUPS:
+                load_group(g + 2)
+            if g < GROUPS:
+                if odd:
+                    square_f32(g)
+                else:
+                    fourth(g)
+            if 0 <= step < CHUNKS:
+                turn_w(step)
+            if odd:
+                if 1 <= g <= GROUPS:
+                    quantise_x_high(g - 1)
+                if g < GROUPS:
+                    square_bf16(g)
+                if 1 <= step <= CHUNKS:
+                    quantise_w(step - 1)
+                if g < GROUPS:
+                    quantise_x_low(g)
+            else:
+                if g + 1 < GROUPS:
+                    regroup_x(g + 1)
+                if g < GROUPS:
+                    cube(g)
+                if 1 <= step <= CHUNKS:
+                    quantise_w(step - 1)
+            if step >= 2:
+                multiply(step - 2)
+            if step - 2 == CHUNKS - 2:
+                for t in range(O_TILES):
+                    invert_denominator(t)
+
+        bias = const.tile([P, O_TILES], F32)
+        nc.vector.tensor_copy(out=bias[:], in_=bias_bf[:])
+        for t in range(O_TILES):
+            finish(t)

@@ -116,11 +116,14 @@ def tile_kanvolutionlayer_k_kernel(tc, x, Wp, bp, Wq, out):
                 in_=x_high[g][:],
             )
 
-        def turn_w(h):
+        def turn_w(h, orders):
             words = w_raw[h][:].bitcast(F32)
-            w_grouped[h] = w_mx.tile([P, W_ROWS * P * PACK], BF16, name="w_grouped", align_bytes=64)
+            if h not in w_grouped:
+                w_grouped[h] = w_mx.tile(
+                    [P, W_ROWS * P * PACK], BF16, name="w_grouped", align_bytes=64
+                )
             grouped_words = w_grouped[h][:].bitcast(F32)
-            for i in range(ORDERS):
+            for i in orders:
                 bank = turned.tile([P, O_TILES, 2, P], F32, name="bank")
                 for t in range(O_TILES):
                     for u in range(2):
@@ -141,21 +144,20 @@ def tile_kanvolutionlayer_k_kernel(tc, x, Wp, bp, Wq, out):
                 out=w_codes[h][:].bitcast(FP8X4), scales=w_scales[h][:], in_=w_grouped[h][:]
             )
 
-        def multiply(h):
+        def multiply(h, t):
             g, s = h // 2, h % 2
-            for t in range(O_TILES):
-                for i in range(ORDERS):
-                    o_cols = slice((i * O_TILES + t) * P, (i * O_TILES + t + 1) * P)
-                    n_cols = slice(i * N, (i + 1) * N)
-                    nc.tensor.matmul_mx(
-                        out=acc[s][t][:],
-                        lhsT=w_codes[h][:, o_cols].bitcast(FP8X4),
-                        lhsT_scale=w_scales[h][:, o_cols],
-                        rhs=x_codes[g][:, n_cols].bitcast(FP8X4),
-                        rhs_scale=x_scales[g][:, n_cols],
-                        start=(g == 0 and i == 0),
-                        stop=(g == GROUPS - 1 and i == ORDERS - 1),
-                    )
+            for i in range(ORDERS):
+                o_cols = slice((i * O_TILES + t) * P, (i * O_TILES + t + 1) * P)
+                n_cols = slice(i * N, (i + 1) * N)
+                nc.tensor.matmul_mx(
+                    out=acc[s][t][:],
+                    lhsT=w_codes[h][:, o_cols].bitcast(FP8X4),
+                    lhsT_scale=w_scales[h][:, o_cols],
+                    rhs=x_codes[g][:, n_cols].bitcast(FP8X4),
+                    rhs_scale=x_scales[g][:, n_cols],
+                    start=(g == 0 and i == 0),
+                    stop=(g == GROUPS - 1 and i == ORDERS - 1),
+                )
 
         def invert_denominator(t):
             size = tail.tile([P, N], F32, name="size")
@@ -202,8 +204,11 @@ def tile_kanvolutionlayer_k_kernel(tc, x, Wp, bp, Wq, out):
                     square_f32(g)
                 else:
                     fourth(g)
-            if 0 <= step < CHUNKS:
-                turn_w(step)
+            for t in range(O_TILES):
+                if 0 <= step < CHUNKS:
+                    turn_w(step, range(2 * t, 2 * t + 2))
+                if step >= 2:
+                    multiply(step - 2, t)
             if odd:
                 if 1 <= g <= GROUPS:
                     quantise_x_high(g - 1)
@@ -220,8 +225,6 @@ def tile_kanvolutionlayer_k_kernel(tc, x, Wp, bp, Wq, out):
                     cube(g)
                 if 1 <= step <= CHUNKS:
                     quantise_w(step - 1)
-            if step >= 2:
-                multiply(step - 2)
             if step - 2 == CHUNKS - 2:
                 for t in range(O_TILES):
                     invert_denominator(t)

@@ -20,6 +20,7 @@ N = BATCH * PIXELS
 O_TILES = OUT_CH // P
 GROUPED = N * PACK
 W_ROWS = ORDERS * O_TILES
+RUN = 4
 CHUNKS = 2 * GROUPS
 
 FLOPS = 2 * 2 * N * OUT_CH * ORDERS * CHANNELS
@@ -79,8 +80,10 @@ def tile_kanvolutionlayer_k_kernel(tc, x, Wp, bp, Wq, out):
         def regroup_x(g):
             x_low[g] = powers.tile([P, 2 * GROUPED], BF16, name="x_low", align_bytes=64)
             nc.vector.tensor_copy(
-                out=x_low[g][:, 0:GROUPED].rearrange("p (b w t) -> p b w t", b=BATCH, t=PACK),
-                in_=x_raw[g][:].rearrange("p b t w -> p b w t"),
+                out=x_low[g][:, 0:GROUPED].rearrange(
+                    "p (b c i t) -> p b c t i", b=BATCH, i=RUN, t=PACK
+                ),
+                in_=x_raw[g][:].rearrange("p b t (c i) -> p b c t i", i=RUN),
             )
 
         def square_f32(g):
@@ -116,14 +119,11 @@ def tile_kanvolutionlayer_k_kernel(tc, x, Wp, bp, Wq, out):
                 in_=x_high[g][:],
             )
 
-        def turn_w(h, orders):
+        def turn_w(h):
             words = w_raw[h][:].bitcast(F32)
-            if h not in w_grouped:
-                w_grouped[h] = w_mx.tile(
-                    [P, W_ROWS * P * PACK], BF16, name="w_grouped", align_bytes=64
-                )
+            w_grouped[h] = w_mx.tile([P, W_ROWS * P * PACK], BF16, name="w_grouped", align_bytes=64)
             grouped_words = w_grouped[h][:].bitcast(F32)
-            for i in orders:
+            for i in range(ORDERS):
                 bank = turned.tile([P, O_TILES, 2, P], F32, name="bank")
                 for t in range(O_TILES):
                     for u in range(2):
@@ -144,20 +144,21 @@ def tile_kanvolutionlayer_k_kernel(tc, x, Wp, bp, Wq, out):
                 out=w_codes[h][:].bitcast(FP8X4), scales=w_scales[h][:], in_=w_grouped[h][:]
             )
 
-        def multiply(h, t):
+        def multiply(h):
             g, s = h // 2, h % 2
-            for i in range(ORDERS):
-                o_cols = slice((i * O_TILES + t) * P, (i * O_TILES + t + 1) * P)
-                n_cols = slice(i * N, (i + 1) * N)
-                nc.tensor.matmul_mx(
-                    out=acc[s][t][:],
-                    lhsT=w_codes[h][:, o_cols].bitcast(FP8X4),
-                    lhsT_scale=w_scales[h][:, o_cols],
-                    rhs=x_codes[g][:, n_cols].bitcast(FP8X4),
-                    rhs_scale=x_scales[g][:, n_cols],
-                    start=(g == 0 and i == 0),
-                    stop=(g == GROUPS - 1 and i == ORDERS - 1),
-                )
+            for t in range(O_TILES):
+                for i in range(ORDERS):
+                    o_cols = slice((i * O_TILES + t) * P, (i * O_TILES + t + 1) * P)
+                    n_cols = slice(i * N, (i + 1) * N)
+                    nc.tensor.matmul_mx(
+                        out=acc[s][t][:],
+                        lhsT=w_codes[h][:, o_cols].bitcast(FP8X4),
+                        lhsT_scale=w_scales[h][:, o_cols],
+                        rhs=x_codes[g][:, n_cols].bitcast(FP8X4),
+                        rhs_scale=x_scales[g][:, n_cols],
+                        start=(g == 0 and i == 0),
+                        stop=(g == GROUPS - 1 and i == ORDERS - 1),
+                    )
 
         def invert_denominator(t):
             size = tail.tile([P, N], F32, name="size")
@@ -204,11 +205,8 @@ def tile_kanvolutionlayer_k_kernel(tc, x, Wp, bp, Wq, out):
                     square_f32(g)
                 else:
                     fourth(g)
-            for t in range(O_TILES):
-                if 0 <= step < CHUNKS:
-                    turn_w(step, range(2 * t, 2 * t + 2))
-                if step >= 2:
-                    multiply(step - 2, t)
+            if 0 <= step < CHUNKS:
+                turn_w(step)
             if odd:
                 if 1 <= g <= GROUPS:
                     quantise_x_high(g - 1)
@@ -225,6 +223,8 @@ def tile_kanvolutionlayer_k_kernel(tc, x, Wp, bp, Wq, out):
                     cube(g)
                 if 1 <= step <= CHUNKS:
                     quantise_w(step - 1)
+            if step >= 2:
+                multiply(step - 2)
             if step - 2 == CHUNKS - 2:
                 for t in range(O_TILES):
                     invert_denominator(t)

@@ -21,6 +21,7 @@ O_TILES = OUT_CH // P
 GROUPED = N * PACK
 W_ROWS = ORDERS * O_TILES
 RUN = 4
+X_AHEAD = 3
 CHUNKS = 2 * GROUPS
 
 FLOPS = 2 * 2 * N * OUT_CH * ORDERS * CHANNELS
@@ -37,7 +38,7 @@ def tile_kanvolutionlayer_k_kernel(tc, x, Wp, bp, Wq, out):
 
     with ExitStack() as ctx:
         const = ctx.enter_context(tc.tile_pool(name="const", bufs=1))
-        x_in = ctx.enter_context(tc.tile_pool(name="x_in", bufs=3))
+        x_in = ctx.enter_context(tc.tile_pool(name="x_in", bufs=4))
         w_in = ctx.enter_context(tc.tile_pool(name="w_in", bufs=6))
         powers = ctx.enter_context(tc.tile_pool(name="powers", bufs=2))
         x_mx = ctx.enter_context(tc.tile_pool(name="x_mx", bufs=3))
@@ -56,7 +57,7 @@ def tile_kanvolutionlayer_k_kernel(tc, x, Wp, bp, Wq, out):
         x_low, x_high, x_sq = {}, {}, {}
         x_codes, x_scales = {}, {}
         w_codes, w_scales, w_grouped = {}, {}, {}
-        inverse = {}
+        root, inverse = {}, {}
 
         def load_x(g):
             x_raw[g] = x_in.tile([P, BATCH, PACK, PIXELS], BF16, name="x_raw")
@@ -71,24 +72,24 @@ def tile_kanvolutionlayer_k_kernel(tc, x, Wp, bp, Wq, out):
             w_raw[h] = w_in.tile([P, W_ROWS, K_PASS], BF16, name="w_raw")
             nc.sync.dma_start(out=w_raw[h][:], in_=w_views[s][:, :, g * K_PASS : (g + 1) * K_PASS])
 
-        def load_group(g):
-            if g + 1 < GROUPS:
-                load_x(g + 1)
-            load_w(2 * g)
-            load_w(2 * g + 1)
+        def batch_ranges(g):
+            return [(b, b + 1) for b in range(BATCH)] if g == 0 else [(0, BATCH)]
 
         def regroup_x(g):
             x_low[g] = powers.tile([P, 2 * GROUPED], BF16, name="x_low", align_bytes=64)
-            nc.vector.tensor_copy(
-                out=x_low[g][:, 0:GROUPED].rearrange(
-                    "p (b c i t) -> p b c t i", b=BATCH, i=RUN, t=PACK
-                ),
-                in_=x_raw[g][:].rearrange("p b t (c i) -> p b c t i", i=RUN),
-            )
+            for b0, b1 in batch_ranges(g):
+                nc.vector.tensor_copy(
+                    out=x_low[g][:, b0 * PIXELS * PACK : b1 * PIXELS * PACK].rearrange(
+                        "p (b c i t) -> p b c t i", b=b1 - b0, i=RUN, t=PACK
+                    ),
+                    in_=x_raw[g][:, b0:b1].rearrange("p b t (c i) -> p b c t i", i=RUN),
+                )
 
         def square_f32(g):
             x_sq[g] = powers.tile([P, GROUPED], F32, name="x_sq")
-            nc.scalar.activation(out=x_sq[g][:], in_=x_low[g][:, 0:GROUPED], func=ACT.Square)
+            for b0, b1 in batch_ranges(g):
+                cols = slice(b0 * PIXELS * PACK, b1 * PIXELS * PACK)
+                nc.scalar.activation(out=x_sq[g][:, cols], in_=x_low[g][:, cols], func=ACT.Square)
 
         def square_bf16(g):
             x1 = x_low[g][:, 0:GROUPED]
@@ -140,33 +141,43 @@ def tile_kanvolutionlayer_k_kernel(tc, x, Wp, bp, Wq, out):
         def quantise_w(h):
             w_codes[h] = w_mx.tile([P, W_ROWS * P], U32, name="w_codes", align_bytes=64)
             w_scales[h] = w_mx.tile([P, W_ROWS * P], U8, name="w_scales", align_bytes=64)
-            nc.vector.quantize_mx(
-                out=w_codes[h][:].bitcast(FP8X4), scales=w_scales[h][:], in_=w_grouped[h][:]
-            )
+            parts = ORDERS if h == CHUNKS - 1 else 1
+            words = W_ROWS * P // parts
+            for i in range(parts):
+                cols = slice(i * words, (i + 1) * words)
+                nc.vector.quantize_mx(
+                    out=w_codes[h][:, cols].bitcast(FP8X4),
+                    scales=w_scales[h][:, cols],
+                    in_=w_grouped[h][:, i * words * PACK : (i + 1) * words * PACK],
+                )
 
         def multiply(h):
             g, s = h // 2, h % 2
-            for t in range(O_TILES):
-                for i in range(ORDERS):
-                    o_cols = slice((i * O_TILES + t) * P, (i * O_TILES + t + 1) * P)
-                    n_cols = slice(i * N, (i + 1) * N)
-                    nc.tensor.matmul_mx(
-                        out=acc[s][t][:],
-                        lhsT=w_codes[h][:, o_cols].bitcast(FP8X4),
-                        lhsT_scale=w_scales[h][:, o_cols],
-                        rhs=x_codes[g][:, n_cols].bitcast(FP8X4),
-                        rhs_scale=x_scales[g][:, n_cols],
-                        start=(g == 0 and i == 0),
-                        stop=(g == GROUPS - 1 and i == ORDERS - 1),
-                    )
+            passes = [(i, t) for i in range(ORDERS) for t in range(O_TILES)]
+            if h == CHUNKS - 2:
+                passes = [(i, t) for t in range(O_TILES) for i in range(ORDERS)]
+            for i, t in passes:
+                o_cols = slice((i * O_TILES + t) * P, (i * O_TILES + t + 1) * P)
+                n_cols = slice(i * N, (i + 1) * N)
+                nc.tensor.matmul_mx(
+                    out=acc[s][t][:],
+                    lhsT=w_codes[h][:, o_cols].bitcast(FP8X4),
+                    lhsT_scale=w_scales[h][:, o_cols],
+                    rhs=x_codes[g][:, n_cols].bitcast(FP8X4),
+                    rhs_scale=x_scales[g][:, n_cols],
+                    start=(g == 0 and i == 0),
+                    stop=(g == GROUPS - 1 and i == ORDERS - 1),
+                )
 
-        def invert_denominator(t):
+        def root_denominator(t):
             size = tail.tile([P, N], F32, name="size")
             nc.scalar.activation(out=size[:], in_=acc[0][t][:], func=ACT.Abs)
-            root = tail.tile([P, N], F32, name="root")
-            nc.scalar.activation(out=root[:], in_=size[:], func=ACT.Abs_reciprocal_sqrt, bias=1.0)
+            root[t] = tail.tile([P, N], F32, name="root")
+            nc.scalar.activation(out=root[t][:], in_=size[:], func=ACT.Abs_reciprocal_sqrt, bias=1.0)
+
+        def invert_denominator(t):
             inverse[t] = tail.tile([P, N], F32, name="inverse")
-            nc.vector.tensor_tensor(out=inverse[t][:], in0=root[:], in1=root[:], op=ALU.mult)
+            nc.vector.tensor_tensor(out=inverse[t][:], in0=root[t][:], in1=root[t][:], op=ALU.mult)
 
         def finish(t):
             result = tail.tile([P, N], F32, name="result")
@@ -181,8 +192,11 @@ def tile_kanvolutionlayer_k_kernel(tc, x, Wp, bp, Wq, out):
             nc.sync.dma_start(out=out_view[t], in_=result[:].rearrange("p (b w) -> p b w", b=BATCH))
 
         load_x(0)
-        load_group(0)
-        load_group(1)
+        load_w(0)
+        for g in range(1, X_AHEAD):
+            load_x(g)
+            load_w(g)
+        load_w(X_AHEAD)
 
         ident = const.tile([P, P], F32)
         make_identity(nc, ident[:])
@@ -195,11 +209,14 @@ def tile_kanvolutionlayer_k_kernel(tc, x, Wp, bp, Wq, out):
         nc.scalar.activation(out=warm[:], in_=ones[:], func=ACT.Abs_reciprocal_sqrt)
 
         regroup_x(0)
-        for step in range(-1, CHUNKS + 2):
+        for step in range(-1, CHUNKS + 1):
             g = (step + 1) // 2
             odd = step % 2 == 1
-            if not odd and g + 2 < GROUPS:
-                load_group(g + 2)
+            if step >= 0:
+                if not odd and step // 2 + X_AHEAD < GROUPS:
+                    load_x(step // 2 + X_AHEAD)
+                if step + X_AHEAD + 1 < CHUNKS:
+                    load_w(step + X_AHEAD + 1)
             if g < GROUPS:
                 if odd:
                     square_f32(g)
@@ -207,27 +224,27 @@ def tile_kanvolutionlayer_k_kernel(tc, x, Wp, bp, Wq, out):
                     fourth(g)
             if 0 <= step < CHUNKS:
                 turn_w(step)
+            if 1 <= step <= CHUNKS:
+                quantise_w(step - 1)
             if odd:
+                if g < GROUPS:
+                    square_bf16(g)
                 if 1 <= g <= GROUPS:
                     quantise_x_high(g - 1)
                 if g < GROUPS:
-                    square_bf16(g)
-                if 1 <= step <= CHUNKS:
-                    quantise_w(step - 1)
-                if g < GROUPS:
                     quantise_x_low(g)
             else:
-                if g + 1 < GROUPS:
-                    regroup_x(g + 1)
                 if g < GROUPS:
                     cube(g)
-                if 1 <= step <= CHUNKS:
-                    quantise_w(step - 1)
-            if step >= 2:
-                multiply(step - 2)
-            if step - 2 == CHUNKS - 2:
+                if g + 1 < GROUPS:
+                    regroup_x(g + 1)
+            if step >= 1:
+                multiply(step - 1)
+            if step - 1 == CHUNKS - 2:
                 for t in range(O_TILES):
-                    invert_denominator(t)
+                    root_denominator(t)
+        for t in range(O_TILES):
+            invert_denominator(t)
 
         bias = const.tile([P, O_TILES], F32)
         nc.vector.tensor_copy(out=bias[:], in_=bias_bf[:])

@@ -57,7 +57,7 @@ def tile_kanvolutionlayer_k_kernel(tc, x, Wp, bp, Wq, out):
         x_low, x_high, x_sq = {}, {}, {}
         x_codes, x_scales = {}, {}
         w_codes, w_scales, w_grouped = {}, {}, {}
-        root, inverse = {}, {}
+        inverse = {}
 
         def load_x(g):
             x_raw[g] = x_in.tile([P, BATCH, PACK, PIXELS], BF16, name="x_raw")
@@ -141,22 +141,13 @@ def tile_kanvolutionlayer_k_kernel(tc, x, Wp, bp, Wq, out):
         def quantise_w(h):
             w_codes[h] = w_mx.tile([P, W_ROWS * P], U32, name="w_codes", align_bytes=64)
             w_scales[h] = w_mx.tile([P, W_ROWS * P], U8, name="w_scales", align_bytes=64)
-            parts = ORDERS if h == CHUNKS - 1 else 1
-            words = W_ROWS * P // parts
-            for i in range(parts):
-                cols = slice(i * words, (i + 1) * words)
-                nc.vector.quantize_mx(
-                    out=w_codes[h][:, cols].bitcast(FP8X4),
-                    scales=w_scales[h][:, cols],
-                    in_=w_grouped[h][:, i * words * PACK : (i + 1) * words * PACK],
-                )
+            nc.vector.quantize_mx(
+                out=w_codes[h][:].bitcast(FP8X4), scales=w_scales[h][:], in_=w_grouped[h][:]
+            )
 
         def multiply(h):
             g, s = h // 2, h % 2
-            passes = [(i, t) for i in range(ORDERS) for t in range(O_TILES)]
-            if h == CHUNKS - 2:
-                passes = [(i, t) for t in range(O_TILES) for i in range(ORDERS)]
-            for i, t in passes:
+            for i, t in [(i, t) for t in range(O_TILES) for i in range(ORDERS)]:
                 o_cols = slice((i * O_TILES + t) * P, (i * O_TILES + t + 1) * P)
                 n_cols = slice(i * N, (i + 1) * N)
                 nc.tensor.matmul_mx(
@@ -169,15 +160,13 @@ def tile_kanvolutionlayer_k_kernel(tc, x, Wp, bp, Wq, out):
                     stop=(g == GROUPS - 1 and i == ORDERS - 1),
                 )
 
-        def root_denominator(t):
+        def invert_denominator(t):
             size = tail.tile([P, N], F32, name="size")
             nc.scalar.activation(out=size[:], in_=acc[0][t][:], func=ACT.Abs)
-            root[t] = tail.tile([P, N], F32, name="root")
-            nc.scalar.activation(out=root[t][:], in_=size[:], func=ACT.Abs_reciprocal_sqrt, bias=1.0)
-
-        def invert_denominator(t):
+            root = tail.tile([P, N], F32, name="root")
+            nc.scalar.activation(out=root[:], in_=size[:], func=ACT.Abs_reciprocal_sqrt, bias=1.0)
             inverse[t] = tail.tile([P, N], F32, name="inverse")
-            nc.vector.tensor_tensor(out=inverse[t][:], in0=root[t][:], in1=root[t][:], op=ALU.mult)
+            nc.scalar.activation(out=inverse[t][:], in_=root[:], func=ACT.Square)
 
         def finish(t):
             result = tail.tile([P, N], F32, name="result")
@@ -209,7 +198,7 @@ def tile_kanvolutionlayer_k_kernel(tc, x, Wp, bp, Wq, out):
         nc.scalar.activation(out=warm[:], in_=ones[:], func=ACT.Abs_reciprocal_sqrt)
 
         regroup_x(0)
-        for step in range(-1, CHUNKS + 1):
+        for step in range(-1, CHUNKS + 2):
             g = (step + 1) // 2
             odd = step % 2 == 1
             if step >= 0:
@@ -224,9 +213,9 @@ def tile_kanvolutionlayer_k_kernel(tc, x, Wp, bp, Wq, out):
                     fourth(g)
             if 0 <= step < CHUNKS:
                 turn_w(step)
-            if 1 <= step <= CHUNKS:
-                quantise_w(step - 1)
             if odd:
+                if 1 <= step <= CHUNKS:
+                    quantise_w(step - 1)
                 if g < GROUPS:
                     square_bf16(g)
                 if 1 <= g <= GROUPS:
@@ -234,17 +223,17 @@ def tile_kanvolutionlayer_k_kernel(tc, x, Wp, bp, Wq, out):
                 if g < GROUPS:
                     quantise_x_low(g)
             else:
-                if g < GROUPS:
-                    cube(g)
                 if g + 1 < GROUPS:
                     regroup_x(g + 1)
-            if step >= 1:
-                multiply(step - 1)
-            if step - 1 == CHUNKS - 2:
+                if 1 <= step <= CHUNKS:
+                    quantise_w(step - 1)
+                if g < GROUPS:
+                    cube(g)
+            if step >= 2:
+                multiply(step - 2)
+            if step - 2 == CHUNKS - 2:
                 for t in range(O_TILES):
-                    root_denominator(t)
-        for t in range(O_TILES):
-            invert_denominator(t)
+                    invert_denominator(t)
 
         bias = const.tile([P, O_TILES], F32)
         nc.vector.tensor_copy(out=bias[:], in_=bias_bf[:])

@@ -57,7 +57,7 @@ def tile_kanvolutionlayer_k_kernel(tc, x, Wp, bp, Wq, out):
         x_low, x_high, x_sq = {}, {}, {}
         x_codes, x_scales = {}, {}
         w_codes, w_scales, w_grouped = {}, {}, {}
-        inverse = {}
+        root, inverse = {}, {}
 
         def load_x(g):
             x_raw[g] = x_in.tile([P, BATCH, PACK, PIXELS], BF16, name="x_raw")
@@ -147,7 +147,9 @@ def tile_kanvolutionlayer_k_kernel(tc, x, Wp, bp, Wq, out):
 
         def multiply(h):
             g, s = h // 2, h % 2
-            for i, t in [(i, t) for t in range(O_TILES) for i in range(ORDERS)]:
+            low = [(i, t) for i in range(ORDERS // 2) for t in range(O_TILES)]
+            high = [(i, t) for t in range(O_TILES) for i in range(ORDERS // 2, ORDERS)]
+            for i, t in low + high:
                 o_cols = slice((i * O_TILES + t) * P, (i * O_TILES + t + 1) * P)
                 n_cols = slice(i * N, (i + 1) * N)
                 nc.tensor.matmul_mx(
@@ -160,13 +162,15 @@ def tile_kanvolutionlayer_k_kernel(tc, x, Wp, bp, Wq, out):
                     stop=(g == GROUPS - 1 and i == ORDERS - 1),
                 )
 
-        def invert_denominator(t):
+        def root_denominator(t):
             size = tail.tile([P, N], F32, name="size")
             nc.scalar.activation(out=size[:], in_=acc[0][t][:], func=ACT.Abs)
-            root = tail.tile([P, N], F32, name="root")
-            nc.scalar.activation(out=root[:], in_=size[:], func=ACT.Abs_reciprocal_sqrt, bias=1.0)
+            root[t] = tail.tile([P, N], F32, name="root")
+            nc.scalar.activation(out=root[t][:], in_=size[:], func=ACT.Abs_reciprocal_sqrt, bias=1.0)
+
+        def invert_denominator(t):
             inverse[t] = tail.tile([P, N], F32, name="inverse")
-            nc.scalar.activation(out=inverse[t][:], in_=root[:], func=ACT.Square)
+            nc.vector.tensor_tensor(out=inverse[t][:], in0=root[t][:], in1=root[t][:], op=ALU.mult)
 
         def finish(t):
             result = tail.tile([P, N], F32, name="result")
@@ -233,9 +237,10 @@ def tile_kanvolutionlayer_k_kernel(tc, x, Wp, bp, Wq, out):
                 multiply(step - 2)
             if step - 2 == CHUNKS - 2:
                 for t in range(O_TILES):
-                    invert_denominator(t)
+                    root_denominator(t)
 
         bias = const.tile([P, O_TILES], F32)
         nc.vector.tensor_copy(out=bias[:], in_=bias_bf[:])
         for t in range(O_TILES):
+            invert_denominator(t)
             finish(t)

@@ -93,7 +93,10 @@ def tile_kanvolutionlayer_k_kernel(tc, x, Wp, bp, Wq, out):
 
         def square_bf16(g):
             x1 = x_low[g][:, 0:GROUPED]
-            nc.vector.tensor_tensor(out=x_low[g][:, GROUPED:], in0=x1, in1=x1, op=ALU.mult)
+            if g == GROUPS - 1:
+                nc.scalar.activation(out=x_low[g][:, GROUPED:], in_=x1, func=ACT.Square)
+            else:
+                nc.vector.tensor_tensor(out=x_low[g][:, GROUPED:], in0=x1, in1=x1, op=ALU.mult)
 
         def fourth(g):
             x_high[g] = powers.tile([P, 2 * GROUPED], BF16, name="x_high", align_bytes=64)
@@ -104,9 +107,11 @@ def tile_kanvolutionlayer_k_kernel(tc, x, Wp, bp, Wq, out):
                 out=x_high[g][:, 0:GROUPED], in0=x_sq[g][:], in1=x_low[g][:, 0:GROUPED], op=ALU.mult
             )
 
-        def quantise_x_low(g):
+        def open_x_mx(g):
             x_codes[g] = x_mx.tile([P, ORDERS * N], U32, name="x_codes", align_bytes=64)
             x_scales[g] = x_mx.tile([P, ORDERS * N], U8, name="x_scales", align_bytes=64)
+
+        def quantise_x_low(g):
             nc.vector.quantize_mx(
                 out=x_codes[g][:, 0 : 2 * N].bitcast(FP8X4),
                 scales=x_scales[g][:, 0 : 2 * N],
@@ -147,9 +152,12 @@ def tile_kanvolutionlayer_k_kernel(tc, x, Wp, bp, Wq, out):
 
         def multiply(h):
             g, s = h // 2, h % 2
-            low = [(i, t) for i in range(ORDERS // 2) for t in range(O_TILES)]
-            high = [(i, t) for t in range(O_TILES) for i in range(ORDERS // 2, ORDERS)]
-            for i, t in low + high:
+            halves = [range(ORDERS // 2), range(ORDERS // 2, ORDERS)]
+            if g == GROUPS - 1:
+                halves = [halves[1], halves[0]]
+            early = [(i, t) for i in halves[0] for t in range(O_TILES)]
+            late = [(i, t) for t in range(O_TILES) for i in halves[1]]
+            for i, t in early + late:
                 o_cols = slice((i * O_TILES + t) * P, (i * O_TILES + t + 1) * P)
                 n_cols = slice(i * N, (i + 1) * N)
                 nc.tensor.matmul_mx(
@@ -159,7 +167,7 @@ def tile_kanvolutionlayer_k_kernel(tc, x, Wp, bp, Wq, out):
                     rhs=x_codes[g][:, n_cols].bitcast(FP8X4),
                     rhs_scale=x_scales[g][:, n_cols],
                     start=(g == 0 and i == 0),
-                    stop=(g == GROUPS - 1 and i == ORDERS - 1),
+                    stop=(g == GROUPS - 1 and i == halves[1][-1]),
                 )
 
         def root_denominator(t):
@@ -193,14 +201,12 @@ def tile_kanvolutionlayer_k_kernel(tc, x, Wp, bp, Wq, out):
 
         ident = const.tile([P, P], F32)
         make_identity(nc, ident[:])
-        bias_bf = const.tile([P, O_TILES], BF16)
-        with nc.allow_non_contiguous_dma(reason="256 bias values, one to a partition"):
-            nc.scalar.dma_start(out=bias_bf[:], in_=bp.rearrange("(t o) -> o t", o=P))
         ones = const.tile([P, 1], F32)
         nc.vector.memset(ones[:], 1.0)
         warm = const.tile([P, 1], F32)
         nc.scalar.activation(out=warm[:], in_=ones[:], func=ACT.Abs_reciprocal_sqrt)
 
+        bias_bf = const.tile([P, O_TILES], BF16)
         regroup_x(0)
         for step in range(-1, CHUNKS + 2):
             g = (step + 1) // 2
@@ -210,29 +216,44 @@ def tile_kanvolutionlayer_k_kernel(tc, x, Wp, bp, Wq, out):
                     load_x(step // 2 + X_AHEAD)
                 if step + X_AHEAD + 1 < CHUNKS:
                     load_w(step + X_AHEAD + 1)
+                if step + X_AHEAD + 1 == CHUNKS:
+                    with nc.allow_non_contiguous_dma(reason="256 bias values, one to a partition"):
+                        nc.sync.dma_start(out=bias_bf[:], in_=bp.rearrange("(t o) -> o t", o=P))
             if g < GROUPS:
                 if odd:
+                    open_x_mx(g)
                     square_f32(g)
                 else:
                     fourth(g)
             if 0 <= step < CHUNKS:
                 turn_w(step)
             if odd:
-                if 1 <= step <= CHUNKS:
+                if 1 <= g < GROUPS:
                     quantise_w(step - 1)
-                if g < GROUPS:
-                    square_bf16(g)
-                if 1 <= g <= GROUPS:
+                    if g < GROUPS - 1:
+                        square_bf16(g)
                     quantise_x_high(g - 1)
-                if g < GROUPS:
+                    if g < GROUPS - 1:
+                        quantise_x_low(g)
+                elif g == 0:
+                    square_bf16(g)
                     quantise_x_low(g)
+                elif g == GROUPS:
+                    quantise_x_high(g - 1)
+                    quantise_w(step - 1)
+                    quantise_x_low(g - 1)
             else:
                 if g + 1 < GROUPS:
                     regroup_x(g + 1)
-                if 1 <= step <= CHUNKS:
-                    quantise_w(step - 1)
-                if g < GROUPS:
+                    if g >= 1:
+                        quantise_w(step - 1)
                     cube(g)
+                elif g < GROUPS:
+                    square_bf16(g)
+                    cube(g)
+                    quantise_w(step - 1)
+                elif g == GROUPS:
+                    quantise_w(step - 1)
             if step >= 2:
                 multiply(step - 2)
             if step - 2 == CHUNKS - 2:

@@ -57,7 +57,7 @@ def tile_kanvolutionlayer_k_kernel(tc, x, Wp, bp, Wq, out):
         x_low, x_high, x_sq = {}, {}, {}
         x_codes, x_scales = {}, {}
         w_codes, w_scales, w_grouped = {}, {}, {}
-        root, inverse = {}, {}
+        size, root, inverse = {}, {}, {}
 
         def load_x(g):
             x_raw[g] = x_in.tile([P, BATCH, PACK, PIXELS], BF16, name="x_raw")
@@ -87,9 +87,17 @@ def tile_kanvolutionlayer_k_kernel(tc, x, Wp, bp, Wq, out):
 
         def square_f32(g):
             x_sq[g] = powers.tile([P, GROUPED], F32, name="x_sq")
-            for b0, b1 in batch_ranges(g):
-                cols = slice(b0 * PIXELS * PACK, b1 * PIXELS * PACK)
-                nc.scalar.activation(out=x_sq[g][:, cols], in_=x_low[g][:, cols], func=ACT.Square)
+            if g == 0:
+                for b in range(BATCH):
+                    nc.scalar.activation(
+                        out=x_sq[g][:, b * PIXELS * PACK : (b + 1) * PIXELS * PACK].rearrange(
+                            "p (n t) -> p n t", t=PACK
+                        ),
+                        in_=x_raw[g][:, b].rearrange("p t n -> p n t"),
+                        func=ACT.Square,
+                    )
+            else:
+                nc.scalar.activation(out=x_sq[g][:], in_=x_low[g][:, 0:GROUPED], func=ACT.Square)
 
         def square_bf16(g):
             x1 = x_low[g][:, 0:GROUPED]
@@ -146,14 +154,20 @@ def tile_kanvolutionlayer_k_kernel(tc, x, Wp, bp, Wq, out):
         def quantise_w(h):
             w_codes[h] = w_mx.tile([P, W_ROWS * P], U32, name="w_codes", align_bytes=64)
             w_scales[h] = w_mx.tile([P, W_ROWS * P], U8, name="w_scales", align_bytes=64)
-            nc.vector.quantize_mx(
-                out=w_codes[h][:].bitcast(FP8X4), scales=w_scales[h][:], in_=w_grouped[h][:]
-            )
+            parts = 2 if h == CHUNKS - 1 else 1
+            words = W_ROWS * P // parts
+            for k in range(parts):
+                cols = slice(k * words, (k + 1) * words)
+                nc.vector.quantize_mx(
+                    out=w_codes[h][:, cols].bitcast(FP8X4),
+                    scales=w_scales[h][:, cols],
+                    in_=w_grouped[h][:, k * words * PACK : (k + 1) * words * PACK],
+                )
 
         def multiply(h):
             g, s = h // 2, h % 2
             halves = [range(ORDERS // 2), range(ORDERS // 2, ORDERS)]
-            if g == GROUPS - 1:
+            if h == CHUNKS - 2:
                 halves = [halves[1], halves[0]]
             early = [(i, t) for i in halves[0] for t in range(O_TILES)]
             late = [(i, t) for t in range(O_TILES) for i in halves[1]]
@@ -170,33 +184,47 @@ def tile_kanvolutionlayer_k_kernel(tc, x, Wp, bp, Wq, out):
                     stop=(g == GROUPS - 1 and i == halves[1][-1]),
                 )
 
+        def size_denominator(t):
+            size[t] = tail.tile([P, N], F32, name="size")
+            nc.scalar.activation(out=size[t][:], in_=acc[0][t][:], func=ACT.Abs)
+
         def root_denominator(t):
-            size = tail.tile([P, N], F32, name="size")
-            nc.scalar.activation(out=size[:], in_=acc[0][t][:], func=ACT.Abs)
             root[t] = tail.tile([P, N], F32, name="root")
-            nc.scalar.activation(out=root[t][:], in_=size[:], func=ACT.Abs_reciprocal_sqrt, bias=1.0)
+            nc.scalar.activation(
+                out=root[t][:], in_=size[t][:], func=ACT.Abs_reciprocal_sqrt, bias=1.0
+            )
 
         def invert_denominator(t):
             inverse[t] = tail.tile([P, N], F32, name="inverse")
-            nc.vector.tensor_tensor(out=inverse[t][:], in0=root[t][:], in1=root[t][:], op=ALU.mult)
+            if t == 0:
+                nc.vector.tensor_tensor(
+                    out=inverse[t][:], in0=root[t][:], in1=root[t][:], op=ALU.mult
+                )
+            else:
+                nc.scalar.activation(out=inverse[t][:], in_=root[t][:], func=ACT.Square)
 
         def finish(t):
             result = tail.tile([P, N], F32, name="result")
-            nc.vector.scalar_tensor_tensor(
-                out=result[:],
-                in0=acc[1][t][:],
-                scalar=bias[:, t : t + 1],
-                in1=inverse[t][:],
-                op0=ALU.add,
-                op1=ALU.mult,
-            )
-            nc.sync.dma_start(out=out_view[t], in_=result[:].rearrange("p (b w) -> p b w", b=BATCH))
+            for b0, b1 in [(0, BATCH)] if t == 0 else [(b, b + 1) for b in range(BATCH)]:
+                cols = slice(b0 * PIXELS, b1 * PIXELS)
+                nc.vector.scalar_tensor_tensor(
+                    out=result[:, cols],
+                    in0=acc[1][t][:, cols],
+                    scalar=bias[:, t : t + 1],
+                    in1=inverse[t][:, cols],
+                    op0=ALU.add,
+                    op1=ALU.mult,
+                )
+                nc.sync.dma_start(
+                    out=out_view[t][:, b0:b1],
+                    in_=result[:, cols].rearrange("p (b w) -> p b w", w=PIXELS),
+                )
 
         load_x(0)
-        load_w(0)
         for g in range(1, X_AHEAD):
             load_x(g)
-            load_w(g)
+            load_w(g - 1)
+        load_w(X_AHEAD - 1)
         load_w(X_AHEAD)
 
         ident = const.tile([P, P], F32)
@@ -229,24 +257,28 @@ def tile_kanvolutionlayer_k_kernel(tc, x, Wp, bp, Wq, out):
                 turn_w(step)
             if odd:
                 if 1 <= g < GROUPS:
+                    if g == 1:
+                        square_bf16(g)
                     quantise_w(step - 1)
-                    if g < GROUPS - 1:
+                    if 1 < g < GROUPS - 1:
                         square_bf16(g)
                     quantise_x_high(g - 1)
                     if g < GROUPS - 1:
                         quantise_x_low(g)
                 elif g == 0:
                     square_bf16(g)
+                    regroup_x(g + 1)
                     quantise_x_low(g)
                 elif g == GROUPS:
                     quantise_x_high(g - 1)
                     quantise_w(step - 1)
                     quantise_x_low(g - 1)
             else:
-                if g + 1 < GROUPS:
+                if g == 0:
+                    cube(g)
+                elif g + 1 < GROUPS:
                     regroup_x(g + 1)
-                    if g >= 1:
-                        quantise_w(step - 1)
+                    quantise_w(step - 1)
                     cube(g)
                 elif g < GROUPS:
                     square_bf16(g)
@@ -258,10 +290,13 @@ def tile_kanvolutionlayer_k_kernel(tc, x, Wp, bp, Wq, out):
                 multiply(step - 2)
             if step - 2 == CHUNKS - 2:
                 for t in range(O_TILES):
+                    size_denominator(t)
+                for t in range(O_TILES):
                     root_denominator(t)
 
         bias = const.tile([P, O_TILES], F32)
         nc.vector.tensor_copy(out=bias[:], in_=bias_bf[:])
         for t in range(O_TILES):
             invert_denominator(t)
+        for t in range(O_TILES):
             finish(t)

@@ -20,7 +20,7 @@ N = BATCH * PIXELS
 O_TILES = OUT_CH // P
 GROUPED = N * PACK
 W_ROWS = ORDERS * O_TILES
-RUN = 4
+RUN = 8
 X_AHEAD = 3
 CHUNKS = 2 * GROUPS
 
@@ -76,7 +76,7 @@ def tile_kanvolutionlayer_k_kernel(tc, x, Wp, bp, Wq, out):
             return [(b, b + 1) for b in range(BATCH)] if g == 0 else [(0, BATCH)]
 
         def regroup_x(g):
-            x_low[g] = powers.tile([P, 2 * GROUPED], BF16, name="x_low", align_bytes=64)
+            x_low[g] = powers.tile([P, 2 * GROUPED], BF16, name="x_low", align_bytes=256)
             for b0, b1 in batch_ranges(g):
                 nc.vector.tensor_copy(
                     out=x_low[g][:, b0 * PIXELS * PACK : b1 * PIXELS * PACK].rearrange(
@@ -107,7 +107,7 @@ def tile_kanvolutionlayer_k_kernel(tc, x, Wp, bp, Wq, out):
                 nc.vector.tensor_tensor(out=x_low[g][:, GROUPED:], in0=x1, in1=x1, op=ALU.mult)
 
         def fourth(g):
-            x_high[g] = powers.tile([P, 2 * GROUPED], BF16, name="x_high", align_bytes=64)
+            x_high[g] = powers.tile([P, 2 * GROUPED], BF16, name="x_high", align_bytes=256)
             nc.scalar.activation(out=x_high[g][:, GROUPED:], in_=x_sq[g][:], func=ACT.Square)
 
         def cube(g):
@@ -116,8 +116,8 @@ def tile_kanvolutionlayer_k_kernel(tc, x, Wp, bp, Wq, out):
             )
 
         def open_x_mx(g):
-            x_codes[g] = x_mx.tile([P, ORDERS * N], U32, name="x_codes", align_bytes=64)
-            x_scales[g] = x_mx.tile([P, ORDERS * N], U8, name="x_scales", align_bytes=64)
+            x_codes[g] = x_mx.tile([P, ORDERS * N], U32, name="x_codes", align_bytes=256)
+            x_scales[g] = x_mx.tile([P, ORDERS * N], U8, name="x_scales", align_bytes=256)
 
         def quantise_x_low(g):
             nc.vector.quantize_mx(
@@ -135,7 +135,7 @@ def tile_kanvolutionlayer_k_kernel(tc, x, Wp, bp, Wq, out):
 
         def turn_w(h):
             words = w_raw[h][:].bitcast(F32)
-            w_grouped[h] = w_mx.tile([P, W_ROWS * P * PACK], BF16, name="w_grouped", align_bytes=64)
+            w_grouped[h] = w_mx.tile([P, W_ROWS * P * PACK], BF16, name="w_grouped", align_bytes=256)
             grouped_words = w_grouped[h][:].bitcast(F32)
             for i in range(ORDERS):
                 bank = turned.tile([P, O_TILES, 2, P], F32, name="bank")
@@ -152,8 +152,8 @@ def tile_kanvolutionlayer_k_kernel(tc, x, Wp, bp, Wq, out):
                 )
 
         def quantise_w(h):
-            w_codes[h] = w_mx.tile([P, W_ROWS * P], U32, name="w_codes", align_bytes=64)
-            w_scales[h] = w_mx.tile([P, W_ROWS * P], U8, name="w_scales", align_bytes=64)
+            w_codes[h] = w_mx.tile([P, W_ROWS * P], U32, name="w_codes", align_bytes=256)
+            w_scales[h] = w_mx.tile([P, W_ROWS * P], U8, name="w_scales", align_bytes=256)
             parts = 2 if h == CHUNKS - 1 else 1
             words = W_ROWS * P // parts
             for k in range(parts):

@@ -99,12 +99,27 @@ def tile_kanvolutionlayer_k_kernel(tc, x, Wp, bp, Wq, out):
             else:
                 nc.scalar.activation(out=x_sq[g][:], in_=x_low[g][:, 0:GROUPED], func=ACT.Square)
 
+        def scalar_squares(g):
+            return GROUPED if g == GROUPS - 1 else GROUPED // 8 if g > 1 else 0
+
+        def square_bf16_scalar(g):
+            n = scalar_squares(g)
+            if n:
+                nc.scalar.activation(
+                    out=x_low[g][:, 2 * GROUPED - n :],
+                    in_=x_low[g][:, GROUPED - n : GROUPED],
+                    func=ACT.Square,
+                )
+
         def square_bf16(g):
-            x1 = x_low[g][:, 0:GROUPED]
-            if g == GROUPS - 1:
-                nc.scalar.activation(out=x_low[g][:, GROUPED:], in_=x1, func=ACT.Square)
-            else:
-                nc.vector.tensor_tensor(out=x_low[g][:, GROUPED:], in0=x1, in1=x1, op=ALU.mult)
+            n = GROUPED - scalar_squares(g)
+            parts = BATCH if g == 0 else 1
+            for k in range(parts):
+                c0, c1 = k * n // parts, (k + 1) * n // parts
+                x1 = x_low[g][:, c0:c1]
+                nc.vector.tensor_tensor(
+                    out=x_low[g][:, GROUPED + c0 : GROUPED + c1], in0=x1, in1=x1, op=ALU.mult
+                )
 
         def fourth(g):
             x_high[g] = powers.tile([P, 2 * GROUPED], BF16, name="x_high", align_bytes=256)
@@ -197,16 +212,18 @@ def tile_kanvolutionlayer_k_kernel(tc, x, Wp, bp, Wq, out):
         def invert_denominator(t):
             inverse[t] = tail.tile([P, N], F32, name="inverse")
             if t == 0:
-                nc.vector.tensor_tensor(
-                    out=inverse[t][:], in0=root[t][:], in1=root[t][:], op=ALU.mult
-                )
+                for b in range(BATCH):
+                    cols = slice(b * PIXELS, (b + 1) * PIXELS)
+                    nc.vector.tensor_tensor(
+                        out=inverse[t][:, cols], in0=root[t][:, cols], in1=root[t][:, cols], op=ALU.mult
+                    )
             else:
                 nc.scalar.activation(out=inverse[t][:], in_=root[t][:], func=ACT.Square)
 
         def finish(t):
             result = tail.tile([P, N], F32, name="result")
-            for b0, b1 in [(0, BATCH)] if t == 0 else [(b, b + 1) for b in range(BATCH)]:
-                cols = slice(b0 * PIXELS, b1 * PIXELS)
+            for b in range(BATCH):
+                cols = slice(b * PIXELS, (b + 1) * PIXELS)
                 nc.vector.scalar_tensor_tensor(
                     out=result[:, cols],
                     in0=acc[1][t][:, cols],
@@ -216,8 +233,8 @@ def tile_kanvolutionlayer_k_kernel(tc, x, Wp, bp, Wq, out):
                     op1=ALU.mult,
                 )
                 nc.sync.dma_start(
-                    out=out_view[t][:, b0:b1],
-                    in_=result[:, cols].rearrange("p (b w) -> p b w", w=PIXELS),
+                    out=out_view[t][:, b],
+                    in_=result[:, cols],
                 )
 
         load_x(0)
@@ -251,6 +268,8 @@ def tile_kanvolutionlayer_k_kernel(tc, x, Wp, bp, Wq, out):
                 if odd:
                     open_x_mx(g)
                     square_f32(g)
+                    if g < GROUPS - 1:
+                        square_bf16_scalar(g)
                 else:
                     fourth(g)
             if 0 <= step < CHUNKS:
@@ -281,7 +300,7 @@ def tile_kanvolutionlayer_k_kernel(tc, x, Wp, bp, Wq, out):
                     quantise_w(step - 1)
                     cube(g)
                 elif g < GROUPS:
-                    square_bf16(g)
+                    square_bf16_scalar(g)
                     cube(g)
                     quantise_w(step - 1)
                 elif g == GROUPS:

@@ -57,7 +57,7 @@ def tile_kanvolutionlayer_k_kernel(tc, x, Wp, bp, Wq, out):
         x_low, x_high, x_sq = {}, {}, {}
         x_codes, x_scales = {}, {}
         w_codes, w_scales, w_grouped = {}, {}, {}
-        size, root, inverse = {}, {}, {}
+        root, inverse = {}, {}
 
         def load_x(g):
             x_raw[g] = x_in.tile([P, BATCH, PACK, PIXELS], BF16, name="x_raw")
@@ -99,23 +99,14 @@ def tile_kanvolutionlayer_k_kernel(tc, x, Wp, bp, Wq, out):
             else:
                 nc.scalar.activation(out=x_sq[g][:], in_=x_low[g][:, 0:GROUPED], func=ACT.Square)
 
-        def scalar_squares(g):
-            return GROUPED if g == GROUPS - 1 else GROUPED // 8 if g > 1 else 0
-
-        def square_bf16_scalar(g):
-            n = scalar_squares(g)
-            if n:
-                nc.scalar.activation(
-                    out=x_low[g][:, 2 * GROUPED - n :],
-                    in_=x_low[g][:, GROUPED - n : GROUPED],
-                    func=ACT.Square,
-                )
-
         def square_bf16(g):
-            n = GROUPED - scalar_squares(g)
-            parts = BATCH if g == 0 else 1
-            for k in range(parts):
-                c0, c1 = k * n // parts, (k + 1) * n // parts
+            if g == GROUPS - 1:
+                nc.scalar.activation(
+                    out=x_low[g][:, GROUPED:], in_=x_low[g][:, 0:GROUPED], func=ACT.Square
+                )
+                return
+            for b0, b1 in batch_ranges(g):
+                c0, c1 = b0 * PIXELS * PACK, b1 * PIXELS * PACK
                 x1 = x_low[g][:, c0:c1]
                 nc.vector.tensor_tensor(
                     out=x_low[g][:, GROUPED + c0 : GROUPED + c1], in0=x1, in1=x1, op=ALU.mult
@@ -199,26 +190,30 @@ def tile_kanvolutionlayer_k_kernel(tc, x, Wp, bp, Wq, out):
                     stop=(g == GROUPS - 1 and i == halves[1][-1]),
                 )
 
-        def size_denominator(t):
-            size[t] = tail.tile([P, N], F32, name="size")
-            nc.scalar.activation(out=size[t][:], in_=acc[0][t][:], func=ACT.Abs)
+        def batch_columns():
+            return [slice(b * PIXELS, (b + 1) * PIXELS) for b in range(BATCH)]
 
         def root_denominator(t):
+            size = tail.tile([P, N], F32, name="size")
             root[t] = tail.tile([P, N], F32, name="root")
-            nc.scalar.activation(
-                out=root[t][:], in_=size[t][:], func=ACT.Abs_reciprocal_sqrt, bias=1.0
-            )
+            for cols in batch_columns():
+                nc.scalar.activation(out=size[:, cols], in_=acc[0][t][:, cols], func=ACT.Abs)
+            for cols in batch_columns():
+                nc.scalar.activation(
+                    out=root[t][:, cols], in_=size[:, cols], func=ACT.Abs_reciprocal_sqrt, bias=1.0
+                )
 
         def invert_denominator(t):
             inverse[t] = tail.tile([P, N], F32, name="inverse")
-            if t == 0:
-                for b in range(BATCH):
-                    cols = slice(b * PIXELS, (b + 1) * PIXELS)
+            for cols in batch_columns():
+                if t == 0:
                     nc.vector.tensor_tensor(
                         out=inverse[t][:, cols], in0=root[t][:, cols], in1=root[t][:, cols], op=ALU.mult
                     )
-            else:
-                nc.scalar.activation(out=inverse[t][:], in_=root[t][:], func=ACT.Square)
+                else:
+                    nc.scalar.activation(
+                        out=inverse[t][:, cols], in_=root[t][:, cols], func=ACT.Square
+                    )
 
         def finish(t):
             result = tail.tile([P, N], F32, name="result")
@@ -268,8 +263,6 @@ def tile_kanvolutionlayer_k_kernel(tc, x, Wp, bp, Wq, out):
                 if odd:
                     open_x_mx(g)
                     square_f32(g)
-                    if g < GROUPS - 1:
-                        square_bf16_scalar(g)
                 else:
                     fourth(g)
             if 0 <= step < CHUNKS:
@@ -300,7 +293,7 @@ def tile_kanvolutionlayer_k_kernel(tc, x, Wp, bp, Wq, out):
                     quantise_w(step - 1)
                     cube(g)
                 elif g < GROUPS:
-                    square_bf16_scalar(g)
+                    square_bf16(g)
                     cube(g)
                     quantise_w(step - 1)
                 elif g == GROUPS:
@@ -308,8 +301,6 @@ def tile_kanvolutionlayer_k_kernel(tc, x, Wp, bp, Wq, out):
             if step >= 2:
                 multiply(step - 2)
             if step - 2 == CHUNKS - 2:
-                for t in range(O_TILES):
-                    size_denominator(t)
                 for t in range(O_TILES):
                     root_denominator(t)
 

from contextlib import ExitStack

import concourse.mybir as mybir
from concourse.masks import make_identity

F32 = mybir.dt.float32
BF16 = mybir.dt.bfloat16
U32 = mybir.dt.uint32
U8 = mybir.dt.uint8
FP8X4 = mybir.dt.float8_e4m3fn_x4
ACT = mybir.ActivationFunctionType
ALU = mybir.AluOpType

BATCH, CHANNELS, OUT_CH, PIXELS, ORDERS = 2, 4096, 256, 256, 4
P = 128
PACK = 4
K_PASS = P * PACK
GROUPS = CHANNELS // K_PASS
N = BATCH * PIXELS
O_TILES = OUT_CH // P
GROUPED = N * PACK
W_ROWS = ORDERS * O_TILES
RUN = 8
X_AHEAD = 3
CHUNKS = 2 * GROUPS

FLOPS = 2 * 2 * N * OUT_CH * ORDERS * CHANNELS


def tile_kanvolutionlayer_k_kernel(tc, x, Wp, bp, Wq, out):
    nc = tc.nc
    x_view = x.rearrange("b (g u p e) h w -> b g p u (e h w)", g=GROUPS, u=2, p=P, e=2)
    w_views = [
        Wq.rearrange("i (t o) c -> o (i t) c", o=P),
        Wp.rearrange("i (t o) c -> o (i t) c", o=P),
    ]
    out_view = out.rearrange("b (t o) h w -> t o b (h w)", o=P)

    with ExitStack() as ctx:
        const = ctx.enter_context(tc.tile_pool(name="const", bufs=1))
        x_in = ctx.enter_context(tc.tile_pool(name="x_in", bufs=4))
        w_in = ctx.enter_context(tc.tile_pool(name="w_in", bufs=6))
        powers = ctx.enter_context(tc.tile_pool(name="powers", bufs=2))
        x_mx = ctx.enter_context(tc.tile_pool(name="x_mx", bufs=3))
        w_mx = ctx.enter_context(tc.tile_pool(name="w_mx", bufs=3))
        tail = ctx.enter_context(tc.tile_pool(name="tail", bufs=2))
        sums = ctx.enter_context(tc.psum_pool(name="sums", bufs=1))
        turned = ctx.enter_context(tc.psum_pool(name="turned", bufs=4))
        ctx.enter_context(tc.manual_schedule())

        acc = [
            [sums.tile([P, N], F32, name="acc_%d_%d" % (s, t)) for t in range(O_TILES)]
            for s in range(2)
        ]

        x_raw, w_raw = {}, {}
        x_low, x_high, x_sq = {}, {}, {}
        x_codes, x_scales = {}, {}
        w_codes, w_scales, w_grouped = {}, {}, {}
        root, inverse = {}, {}

        def load_x(g):
            x_raw[g] = x_in.tile([P, BATCH, PACK, PIXELS], BF16, name="x_raw")
            for b in range(BATCH):
                nc.sync.dma_start(
                    out=x_raw[g][:, b].rearrange("p (u e) w -> p u (e w)", u=2),
                    in_=x_view[b, g],
                )

        def load_w(h):
            g, s = h // 2, h % 2
            w_raw[h] = w_in.tile([P, W_ROWS, K_PASS], BF16, name="w_raw")
            nc.sync.dma_start(out=w_raw[h][:], in_=w_views[s][:, :, g * K_PASS : (g + 1) * K_PASS])

        def batch_ranges(g):
            return [(b, b + 1) for b in range(BATCH)] if g == 0 else [(0, BATCH)]

        def regroup_x(g):
            x_low[g] = powers.tile([P, 2 * GROUPED], BF16, name="x_low", align_bytes=256)
            for b0, b1 in batch_ranges(g):
                nc.vector.tensor_copy(
                    out=x_low[g][:, b0 * PIXELS * PACK : b1 * PIXELS * PACK].rearrange(
                        "p (b c i t) -> p b c t i", b=b1 - b0, i=RUN, t=PACK
                    ),
                    in_=x_raw[g][:, b0:b1].rearrange("p b t (c i) -> p b c t i", i=RUN),
                )

        def square_f32(g):
            x_sq[g] = powers.tile([P, GROUPED], F32, name="x_sq")
            if g == 0:
                for b in range(BATCH):
                    nc.scalar.activation(
                        out=x_sq[g][:, b * PIXELS * PACK : (b + 1) * PIXELS * PACK].rearrange(
                            "p (n t) -> p n t", t=PACK
                        ),
                        in_=x_raw[g][:, b].rearrange("p t n -> p n t"),
                        func=ACT.Square,
                    )
            else:
                nc.scalar.activation(out=x_sq[g][:], in_=x_low[g][:, 0:GROUPED], func=ACT.Square)

        def square_bf16(g):
            if g == GROUPS - 1:
                nc.scalar.activation(
                    out=x_low[g][:, GROUPED:], in_=x_low[g][:, 0:GROUPED], func=ACT.Square
                )
                return
            for b0, b1 in batch_ranges(g):
                c0, c1 = b0 * PIXELS * PACK, b1 * PIXELS * PACK
                x1 = x_low[g][:, c0:c1]
                nc.vector.tensor_tensor(
                    out=x_low[g][:, GROUPED + c0 : GROUPED + c1], in0=x1, in1=x1, op=ALU.mult
                )

        def fourth(g):
            x_high[g] = powers.tile([P, 2 * GROUPED], BF16, name="x_high", align_bytes=256)
            nc.scalar.activation(out=x_high[g][:, GROUPED:], in_=x_sq[g][:], func=ACT.Square)

        def cube(g):
            nc.vector.tensor_tensor(
                out=x_high[g][:, 0:GROUPED], in0=x_sq[g][:], in1=x_low[g][:, 0:GROUPED], op=ALU.mult
            )

        def open_x_mx(g):
            x_codes[g] = x_mx.tile([P, ORDERS * N], U32, name="x_codes", align_bytes=256)
            x_scales[g] = x_mx.tile([P, ORDERS * N], U8, name="x_scales", align_bytes=256)

        def quantise_x_low(g):
            nc.vector.quantize_mx(
                out=x_codes[g][:, 0 : 2 * N].bitcast(FP8X4),
                scales=x_scales[g][:, 0 : 2 * N],
                in_=x_low[g][:],
            )

        def quantise_x_high(g):
            nc.vector.quantize_mx(
                out=x_codes[g][:, 2 * N :].bitcast(FP8X4),
                scales=x_scales[g][:, 2 * N :],
                in_=x_high[g][:],
            )

        def turn_w(h):
            words = w_raw[h][:].bitcast(F32)
            w_grouped[h] = w_mx.tile([P, W_ROWS * P * PACK], BF16, name="w_grouped", align_bytes=256)
            grouped_words = w_grouped[h][:].bitcast(F32)
            for i in range(ORDERS):
                bank = turned.tile([P, O_TILES, 2, P], F32, name="bank")
                for t in range(O_TILES):
                    for u in range(2):
                        nc.tensor.transpose(
                            bank[:, t, u, :], words[:, i * O_TILES + t, u * P : (u + 1) * P], ident[:]
                        )
                nc.scalar.copy(
                    out=grouped_words[:, i * N : (i + 1) * N].rearrange(
                        "p (t o u) -> p t o u", t=O_TILES, u=2
                    ),
                    in_=bank[:].rearrange("p t u o -> p t o u"),
                )

        def quantise_w(h):
            w_codes[h] = w_mx.tile([P, W_ROWS * P], U32, name="w_codes", align_bytes=256)
            w_scales[h] = w_mx.tile([P, W_ROWS * P], U8, name="w_scales", align_bytes=256)
            parts = 2 if h == CHUNKS - 1 else 1
            words = W_ROWS * P // parts
            for k in range(parts):
                cols = slice(k * words, (k + 1) * words)
                nc.vector.quantize_mx(
                    out=w_codes[h][:, cols].bitcast(FP8X4),
                    scales=w_scales[h][:, cols],
                    in_=w_grouped[h][:, k * words * PACK : (k + 1) * words * PACK],
                )

        def multiply(h):
            g, s = h // 2, h % 2
            halves = [range(ORDERS // 2), range(ORDERS // 2, ORDERS)]
            if h == CHUNKS - 2:
                halves = [halves[1], halves[0]]
            early = [(i, t) for i in halves[0] for t in range(O_TILES)]
            late = [(i, t) for t in range(O_TILES) for i in halves[1]]
            for i, t in early + late:
                o_cols = slice((i * O_TILES + t) * P, (i * O_TILES + t + 1) * P)
                n_cols = slice(i * N, (i + 1) * N)
                nc.tensor.matmul_mx(
                    out=acc[s][t][:],
                    lhsT=w_codes[h][:, o_cols].bitcast(FP8X4),
                    lhsT_scale=w_scales[h][:, o_cols],
                    rhs=x_codes[g][:, n_cols].bitcast(FP8X4),
                    rhs_scale=x_scales[g][:, n_cols],
                    start=(g == 0 and i == 0),
                    stop=(g == GROUPS - 1 and i == halves[1][-1]),
                )

        def batch_columns():
            return [slice(b * PIXELS, (b + 1) * PIXELS) for b in range(BATCH)]

        def root_denominator(t):
            size = tail.tile([P, N], F32, name="size")
            root[t] = tail.tile([P, N], F32, name="root")
            for cols in batch_columns():
                nc.scalar.activation(out=size[:, cols], in_=acc[0][t][:, cols], func=ACT.Abs)
            for cols in batch_columns():
                nc.scalar.activation(
                    out=root[t][:, cols], in_=size[:, cols], func=ACT.Abs_reciprocal_sqrt, bias=1.0
                )

        def invert_denominator(t):
            inverse[t] = tail.tile([P, N], F32, name="inverse")
            for cols in batch_columns():
                if t == 0:
                    nc.vector.tensor_tensor(
                        out=inverse[t][:, cols], in0=root[t][:, cols], in1=root[t][:, cols], op=ALU.mult
                    )
                else:
                    nc.scalar.activation(
                        out=inverse[t][:, cols], in_=root[t][:, cols], func=ACT.Square
                    )

        def finish(t):
            result = tail.tile([P, N], F32, name="result")
            for b in range(BATCH):
                cols = slice(b * PIXELS, (b + 1) * PIXELS)
                nc.vector.scalar_tensor_tensor(
                    out=result[:, cols],
                    in0=acc[1][t][:, cols],
                    scalar=bias[:, t : t + 1],
                    in1=inverse[t][:, cols],
                    op0=ALU.add,
                    op1=ALU.mult,
                )
                nc.sync.dma_start(
                    out=out_view[t][:, b],
                    in_=result[:, cols],
                )

        load_x(0)
        for g in range(1, X_AHEAD):
            load_x(g)
            load_w(g - 1)
        load_w(X_AHEAD - 1)
        load_w(X_AHEAD)

        ident = const.tile([P, P], F32)
        make_identity(nc, ident[:])
        ones = const.tile([P, 1], F32)
        nc.vector.memset(ones[:], 1.0)
        warm = const.tile([P, 1], F32)
        nc.scalar.activation(out=warm[:], in_=ones[:], func=ACT.Abs_reciprocal_sqrt)

        bias_bf = const.tile([P, O_TILES], BF16)
        regroup_x(0)
        for step in range(-1, CHUNKS + 2):
            g = (step + 1) // 2
            odd = step % 2 == 1
            if step >= 0:
                if not odd and step // 2 + X_AHEAD < GROUPS:
                    load_x(step // 2 + X_AHEAD)
                if step + X_AHEAD + 1 < CHUNKS:
                    load_w(step + X_AHEAD + 1)
                if step + X_AHEAD + 1 == CHUNKS:
                    with nc.allow_non_contiguous_dma(reason="256 bias values, one to a partition"):
                        nc.sync.dma_start(out=bias_bf[:], in_=bp.rearrange("(t o) -> o t", o=P))
            if g < GROUPS:
                if odd:
                    open_x_mx(g)
                    square_f32(g)
                else:
                    fourth(g)
            if 0 <= step < CHUNKS:
                turn_w(step)
            if odd:
                if 1 <= g < GROUPS:
                    if g == 1:
                        square_bf16(g)
                    quantise_w(step - 1)
                    if 1 < g < GROUPS - 1:
                        square_bf16(g)
                    quantise_x_high(g - 1)
                    if g < GROUPS - 1:
                        quantise_x_low(g)
                elif g == 0:
                    square_bf16(g)
                    regroup_x(g + 1)
                    quantise_x_low(g)
                elif g == GROUPS:
                    quantise_x_high(g - 1)
                    quantise_w(step - 1)
                    quantise_x_low(g - 1)
            else:
                if g == 0:
                    cube(g)
                elif g + 1 < GROUPS:
                    regroup_x(g + 1)
                    quantise_w(step - 1)
                    cube(g)
                elif g < GROUPS:
                    square_bf16(g)
                    cube(g)
                    quantise_w(step - 1)
                elif g == GROUPS:
                    quantise_w(step - 1)
            if step >= 2:
                multiply(step - 2)
            if step - 2 == CHUNKS - 2:
                for t in range(O_TILES):
                    root_denominator(t)

        bias = const.tile([P, O_TILES], F32)
        nc.vector.tensor_copy(out=bias[:], in_=bias_bf[:])
        for t in range(O_TILES):
            invert_denominator(t)
        for t in range(O_TILES):
            finish(t)
